import numpy as np
import ml_dtypes


def mxq(x, axis, fmt="e4m3"):
    dtype, down = {"e4m3": (ml_dtypes.float8_e4m3fn, 7), "e5m2": (ml_dtypes.float8_e5m2, 14)}[fmt]
    v = np.moveaxis(np.asarray(x, np.float32).astype(ml_dtypes.bfloat16).astype(np.float64), axis, -1)
    blocks = v.reshape(v.shape[:-1] + (-1, 32))
    amax = np.abs(blocks).max(-1, keepdims=True)
    byte = np.maximum(np.where(amax > 0, np.frexp(amax)[1] - 1 + 127, 0) - down, 1)
    scale = np.exp2(byte - 127.0)
    codes = (blocks / scale).astype(np.float32).astype(dtype).astype(np.float64)
    return np.moveaxis((codes * scale).reshape(v.shape), -1, axis)


WIDE = False


def mx_kscale(k):
    if not WIDE:
        return np.ones(k)
    levels = np.array([20, -20, 10, -10, 0])
    a = np.random.permutation(np.resize(levels, k // 512 * 4)).reshape(k // 512, 4)
    idx = np.arange(k)
    return np.exp2(a[idx // 512, idx % 128 // 32])


BF16 = ml_dtypes.bfloat16


def bf(x):
    return np.asarray(x, np.float32).astype(BF16)


def f64(x):
    return np.asarray(x).astype(np.float64)


B, N, I, O = 128, 12, 128, 512
WS = 0.7 / np.sqrt(I)
GS = 16.0


def setup_inputs():
    u = mx_kscale(O)
    x = np.random.standard_normal((B, N, I)).reshape(B, N * I)
    w_self = np.random.standard_normal((N, O, I)) * WS / u[:, None]
    w_parent = np.random.standard_normal((N - 1, O, I)) * WS / u[:, None]
    bias = np.random.standard_normal(N * O) * 0.5
    g = np.random.standard_normal((B, N, O)) * np.exp2(np.random.randint(-12, 1, (B, 1, 1))) * GS * u
    return {"x": bf(x), "w_self": bf(w_self), "w_parent": bf(w_parent), "bias": bf(bias),
            "grad_out": bf(g.reshape(B, N * O))}


def reference(x, w_self, w_parent, bias, grad_out):
    gq = mxq(f64(grad_out).reshape(B, N, O).transpose(1, 0, 2), 2, "e5m2")
    d_self = gq @ mxq(f64(w_self), 1, "e4m3")
    d_par = gq[1:] @ mxq(f64(w_parent), 1, "e4m3")
    d = np.concatenate([d_self[:-1] + d_par, d_self[-1:]], 0)
    return d.transpose(1, 0, 2).reshape(B, N * I)

@@ -1,0 +1,138 @@
+from contextlib import ExitStack
+
+import concourse.mybir as mybir
+from concourse.masks import make_identity
+
+BF16 = mybir.dt.bfloat16
+F32 = mybir.dt.float32
+I32 = mybir.dt.int32
+U32 = mybir.dt.uint32
+U8 = mybir.dt.uint8
+E4M3_X4 = mybir.dt.float8_e4m3fn_x4
+E5M2_X4 = mybir.dt.float8_e5m2_x4
+
+P = 128
+PACK = 4
+JOINTS = 12
+K = P * PACK
+BLOCK = 128
+BANK_JOINTS = 4
+BANKS = JOINTS // BANK_JOINTS
+WINDOW = BANK_JOINTS * BLOCK
+GAP = (BANK_JOINTS - 1) * BLOCK
+PERIOD = 2 * BLOCK + GAP
+PARENT, SELF = 0, 1
+
+FLOPS = 2 * P * K * BLOCK * (2 * JOINTS - 1)
+BYTES = 2 * (2 * JOINTS - 1) * K * BLOCK + 2 * P * JOINTS * K + 4 * P * JOINTS * BLOCK
+
+
+def tile_skeletonlinear_pa_s_kernel(tc, x, w_self, w_parent, bias, grad_out, out):
+    nc = tc.nc
+    with ExitStack() as ctx:
+        keep = ctx.enter_context(tc.tile_pool(name="keep", bufs=1))
+        turn_psum = ctx.enter_context(tc.psum_pool(name="turn_psum", bufs=4))
+        acc_psum = ctx.enter_context(tc.psum_pool(name="acc_psum", bufs=BANKS))
+
+        g_raw = keep.tile([P, JOINTS * K], BF16)
+        g_grouped = keep.tile([P, JOINTS, P, PACK], BF16, align_bytes=64)
+        g_codes = keep.tile([P, JOINTS, P], U32, align_bytes=64)
+        g_scales = keep.tile([P, JOINTS, P], U8, align_bytes=64)
+        w_raw = keep.tile([P, JOINTS, 2, K], BF16)
+        w_grouped = keep.tile([P, JOINTS, 2, BLOCK, PACK], BF16, align_bytes=64)
+        w_codes = keep.tile([P, JOINTS * PERIOD], U32, align_bytes=64)
+        w_scales = keep.tile([P, JOINTS * PERIOD], U8, align_bytes=64)
+        out_sb = keep.tile([P, JOINTS * BLOCK], F32)
+        identity = keep.tile([P, P], F32)
+
+        for bank in range(BANKS):
+            g_cols = slice(bank * BANK_JOINTS * K, (bank + 1) * BANK_JOINTS * K)
+            nc.sync.dma_start(out=g_raw[:, g_cols], in_=grad_out[:, g_cols])
+            for first in range(bank * BANK_JOINTS, (bank + 1) * BANK_JOINTS, 2):
+                nc.sync.dma_start(
+                    out=w_raw[:, first : first + 2, SELF, :],
+                    in_=w_self[first : first + 2].rearrange("n (p t) i -> p n (t i)", t=PACK),
+                )
+                has_parent = max(first, 1)
+                nc.sync.dma_start(
+                    out=w_raw[:, has_parent : first + 2, PARENT, :],
+                    in_=w_parent[has_parent - 1 : first + 1].rearrange(
+                        "n (p t) i -> p n (t i)", t=PACK
+                    ),
+                )
+
+        code_gaps = w_codes[:].bitcast(I32).rearrange("p (n w) -> p n w", w=PERIOD)
+        nc.vector.memset(code_gaps[:, 0 : JOINTS - 1, 2 * BLOCK : PERIOD], 0)
+        scale_gaps = w_scales[:].bitcast(I32).rearrange("p (n w) -> p n w", w=PERIOD // 4)
+        nc.vector.memset(scale_gaps[:, 0 : JOINTS - 1, 2 * BLOCK // 4 : PERIOD // 4], 0)
+        make_identity(nc, identity[:])
+
+        g_words = g_raw[:].bitcast(F32).rearrange("b (n q u) -> b n u q", n=JOINTS, u=2)
+        g_grouped_words = g_grouped[:].bitcast(F32)
+
+        def quantise_g(first):
+            pair = slice(first, first + 2)
+            turned = turn_psum.tile([P, 2, 2, P], F32)
+            for j in range(2):
+                for u in range(2):
+                    nc.tensor.transpose(turned[:, j, u, :], g_words[:, first + j, u, :], identity[:])
+            nc.scalar.copy(
+                out=g_grouped_words[:, pair, :, :], in_=turned[:].rearrange("p n u b -> p n b u")
+            )
+            nc.vector.quantize_mx(
+                out=g_codes[:, pair, :].rearrange("p n b -> p (n b)").bitcast(E5M2_X4),
+                scales=g_scales[:, pair, :].rearrange("p n b -> p (n b)"),
+                in_=g_grouped[:, pair].rearrange("p n b t -> p (n b t)"),
+            )
+
+        def quantise_w(n):
+            blocks = slice(PARENT if n > 0 else SELF, SELF + 1)
+            if n % 3 == 1:
+                for s in range(2):
+                    nc.scalar.copy(
+                        out=w_grouped[:, n, s].rearrange("p (c r) t -> p c t r", r=4),
+                        in_=w_raw[:, n, s].rearrange("p (t c r) -> p c t r", t=PACK, r=4),
+                    )
+            else:
+                nc.vector.tensor_copy(
+                    out=w_grouped[:, n, blocks].rearrange("p s (c r) t -> p s c t r", r=4),
+                    in_=w_raw[:, n, blocks].rearrange("p s (t c r) -> p s c t r", t=PACK, r=4),
+                )
+            cols = slice(n * PERIOD + (0 if n > 0 else BLOCK), n * PERIOD + 2 * BLOCK)
+            nc.vector.quantize_mx(
+                out=w_codes[:, cols].bitcast(E4M3_X4),
+                scales=w_scales[:, cols],
+                in_=w_grouped[:, n, blocks].rearrange("p s i t -> p (s i t)"),
+            )
+
+        def multiply(acc, n, first_col, start, stop):
+            window = slice(first_col, first_col + WINDOW)
+            nc.tensor.matmul_mx(
+                out=acc[:],
+                lhsT=g_codes[:, n, :].bitcast(E5M2_X4),
+                lhsT_scale=g_scales[:, n, :],
+                rhs=w_codes[:, window].bitcast(E4M3_X4),
+                rhs_scale=w_scales[:, window],
+                start=start,
+                stop=stop,
+            )
+
+        def store(acc, bank):
+            cols = slice(bank * WINDOW, (bank + 1) * WINDOW)
+            nc.scalar.copy(out=out_sb[:, cols], in_=acc[:])
+            nc.sync.dma_start(out=out[:, cols], in_=out_sb[:, cols])
+
+        acc = None
+        for n in range(JOINTS):
+            place = n % BANK_JOINTS
+            if n % 2 == 0:
+                quantise_g(n)
+            quantise_w(n)
+            self_col = n * PERIOD + BLOCK
+            if place == 0:
+                if n > 0:
+                    multiply(acc, n, self_col - WINDOW, start=False, stop=True)
+                    store(acc, n // BANK_JOINTS - 1)
+                acc = acc_psum.tile([P, WINDOW], F32)
+            multiply(acc, n, self_col - place * BLOCK, start=(place == 0), stop=(n == JOINTS - 1))
+        store(acc, BANKS - 1)

@@ -22,6 +22,7 @@ WINDOW = BANK_JOINTS * BLOCK
 GAP = (BANK_JOINTS - 1) * BLOCK
 PERIOD = 2 * BLOCK + GAP
 PARENT, SELF = 0, 1
+PAIRS = JOINTS // 2
 
 FLOPS = 2 * P * K * BLOCK * (2 * JOINTS - 1)
 BYTES = 2 * (2 * JOINTS - 1) * K * BLOCK + 2 * P * JOINTS * K + 4 * P * JOINTS * BLOCK
@@ -33,6 +34,7 @@ def tile_skeletonlinear_pa_s_kernel(tc, x, w_self, w_parent, bias, grad_out, out
         keep = ctx.enter_context(tc.tile_pool(name="keep", bufs=1))
         turn_psum = ctx.enter_context(tc.psum_pool(name="turn_psum", bufs=4))
         acc_psum = ctx.enter_context(tc.psum_pool(name="acc_psum", bufs=BANKS))
+        ctx.enter_context(tc.manual_schedule())
 
         g_raw = keep.tile([P, JOINTS * K], BF16)
         g_grouped = keep.tile([P, JOINTS, P, PACK], BF16, align_bytes=64)
@@ -45,21 +47,18 @@ def tile_skeletonlinear_pa_s_kernel(tc, x, w_self, w_parent, bias, grad_out, out
         out_sb = keep.tile([P, JOINTS * BLOCK], F32)
         identity = keep.tile([P, P], F32)
 
-        for bank in range(BANKS):
-            g_cols = slice(bank * BANK_JOINTS * K, (bank + 1) * BANK_JOINTS * K)
+        for first in range(0, JOINTS, 2):
+            g_cols = slice(first * K, (first + 2) * K)
             nc.sync.dma_start(out=g_raw[:, g_cols], in_=grad_out[:, g_cols])
-            for first in range(bank * BANK_JOINTS, (bank + 1) * BANK_JOINTS, 2):
-                nc.sync.dma_start(
-                    out=w_raw[:, first : first + 2, SELF, :],
-                    in_=w_self[first : first + 2].rearrange("n (p t) i -> p n (t i)", t=PACK),
-                )
-                has_parent = max(first, 1)
-                nc.sync.dma_start(
-                    out=w_raw[:, has_parent : first + 2, PARENT, :],
-                    in_=w_parent[has_parent - 1 : first + 1].rearrange(
-                        "n (p t) i -> p n (t i)", t=PACK
-                    ),
-                )
+            has_parent = max(first, 1)
+            nc.sync.dma_start(
+                out=w_raw[:, has_parent : first + 2, PARENT, :],
+                in_=w_parent[has_parent - 1 : first + 1].rearrange("n (p t) i -> p n (t i)", t=PACK),
+            )
+            nc.sync.dma_start(
+                out=w_raw[:, first : first + 2, SELF, :],
+                in_=w_self[first : first + 2].rearrange("n (p t) i -> p n (t i)", t=PACK),
+            )
 
         code_gaps = w_codes[:].bitcast(I32).rearrange("p (n w) -> p n w", w=PERIOD)
         nc.vector.memset(code_gaps[:, 0 : JOINTS - 1, 2 * BLOCK : PERIOD], 0)
@@ -70,15 +69,33 @@ def tile_skeletonlinear_pa_s_kernel(tc, x, w_self, w_parent, bias, grad_out, out
         g_words = g_raw[:].bitcast(F32).rearrange("b (n q u) -> b n u q", n=JOINTS, u=2)
         g_grouped_words = g_grouped[:].bitcast(F32)
 
-        def quantise_g(first):
-            pair = slice(first, first + 2)
+        def transpose_g(first):
             turned = turn_psum.tile([P, 2, 2, P], F32)
             for j in range(2):
                 for u in range(2):
                     nc.tensor.transpose(turned[:, j, u, :], g_words[:, first + j, u, :], identity[:])
+            return turned
+
+        def group_g(first, turned):
             nc.scalar.copy(
-                out=g_grouped_words[:, pair, :, :], in_=turned[:].rearrange("p n u b -> p n b u")
+                out=g_grouped_words[:, first : first + 2, :, :],
+                in_=turned[:].rearrange("p n u b -> p n b u"),
             )
+
+        def group_w(first):
+            pair = slice(first, first + 2)
+            nc.vector.tensor_copy(
+                out=w_grouped[:, pair, SELF].rearrange("p n (c r) t -> p n c t r", r=4),
+                in_=w_raw[:, pair, SELF].rearrange("p n (t c r) -> p n c t r", t=PACK, r=4),
+            )
+            for n in range(max(first, 1), first + 2):
+                nc.scalar.copy(
+                    out=w_grouped[:, n, PARENT].rearrange("p (c r) t -> p c t r", r=4),
+                    in_=w_raw[:, n, PARENT].rearrange("p (t c r) -> p c t r", t=PACK, r=4),
+                )
+
+        def quantise_g(first):
+            pair = slice(first, first + 2)
             nc.vector.quantize_mx(
                 out=g_codes[:, pair, :].rearrange("p n b -> p (n b)").bitcast(E5M2_X4),
                 scales=g_scales[:, pair, :].rearrange("p n b -> p (n b)"),
@@ -87,17 +104,6 @@ def tile_skeletonlinear_pa_s_kernel(tc, x, w_self, w_parent, bias, grad_out, out
 
         def quantise_w(n):
             blocks = slice(PARENT if n > 0 else SELF, SELF + 1)
-            if n % 3 == 1:
-                for s in range(2):
-                    nc.scalar.copy(
-                        out=w_grouped[:, n, s].rearrange("p (c r) t -> p c t r", r=4),
-                        in_=w_raw[:, n, s].rearrange("p (t c r) -> p c t r", t=PACK, r=4),
-                    )
-            else:
-                nc.vector.tensor_copy(
-                    out=w_grouped[:, n, blocks].rearrange("p s (c r) t -> p s c t r", r=4),
-                    in_=w_raw[:, n, blocks].rearrange("p s (t c r) -> p s c t r", t=PACK, r=4),
-                )
             cols = slice(n * PERIOD + (0 if n > 0 else BLOCK), n * PERIOD + 2 * BLOCK)
             nc.vector.quantize_mx(
                 out=w_codes[:, cols].bitcast(E4M3_X4),
@@ -119,20 +125,31 @@ def tile_skeletonlinear_pa_s_kernel(tc, x, w_self, w_parent, bias, grad_out, out
 
         def store(acc, bank):
             cols = slice(bank * WINDOW, (bank + 1) * WINDOW)
-            nc.scalar.copy(out=out_sb[:, cols], in_=acc[:])
+            nc.vector.tensor_copy(out=out_sb[:, cols], in_=acc[:])
             nc.sync.dma_start(out=out[:, cols], in_=out_sb[:, cols])
 
         acc = None
-        for n in range(JOINTS):
-            place = n % BANK_JOINTS
-            if n % 2 == 0:
-                quantise_g(n)
-            quantise_w(n)
-            self_col = n * PERIOD + BLOCK
-            if place == 0:
-                if n > 0:
-                    multiply(acc, n, self_col - WINDOW, start=False, stop=True)
-                    store(acc, n // BANK_JOINTS - 1)
-                acc = acc_psum.tile([P, WINDOW], F32)
-            multiply(acc, n, self_col - place * BLOCK, start=(place == 0), stop=(n == JOINTS - 1))
+        full = None
+        turned = transpose_g(0)
+        group_g(0, turned)
+        for first in range(0, JOINTS, 2):
+            if first + 2 < JOINTS:
+                turned = transpose_g(first + 2)
+            group_w(first)
+            if first + 2 < JOINTS:
+                group_g(first + 2, turned)
+            if full is not None:
+                store(full, first // BANK_JOINTS - 1)
+                full = None
+            quantise_g(first)
+            for n in (first, first + 1):
+                quantise_w(n)
+                place = n % BANK_JOINTS
+                self_col = n * PERIOD + BLOCK
+                if place == 0:
+                    if n > 0:
+                        multiply(acc, n, self_col - WINDOW, start=False, stop=True)
+                        full = acc
+                    acc = acc_psum.tile([P, WINDOW], F32)
+                multiply(acc, n, self_col - place * BLOCK, start=(place == 0), stop=(n == JOINTS - 1))
         store(acc, BANKS - 1)

@@ -16,13 +16,11 @@ PACK = 4
 JOINTS = 12
 K = P * PACK
 BLOCK = 128
-BANK_JOINTS = 4
-BANKS = JOINTS // BANK_JOINTS
-WINDOW = BANK_JOINTS * BLOCK
-GAP = (BANK_JOINTS - 1) * BLOCK
-PERIOD = 2 * BLOCK + GAP
+WINDOW = 4 * BLOCK
+PERIOD = 3 * BLOCK
+LEAD = BLOCK
+UNREAD = 2 * BLOCK
 PARENT, SELF = 0, 1
-PAIRS = JOINTS // 2
 
 FLOPS = 2 * P * K * BLOCK * (2 * JOINTS - 1)
 BYTES = 2 * (2 * JOINTS - 1) * K * BLOCK + 2 * P * JOINTS * K + 4 * P * JOINTS * BLOCK
@@ -33,7 +31,7 @@ def tile_skeletonlinear_pa_s_kernel(tc, x, w_self, w_parent, bias, grad_out, out
     with ExitStack() as ctx:
         keep = ctx.enter_context(tc.tile_pool(name="keep", bufs=1))
         turn_psum = ctx.enter_context(tc.psum_pool(name="turn_psum", bufs=4))
-        acc_psum = ctx.enter_context(tc.psum_pool(name="acc_psum", bufs=BANKS))
+        acc_psum = ctx.enter_context(tc.psum_pool(name="acc_psum", bufs=4))
         ctx.enter_context(tc.manual_schedule())
 
         g_raw = keep.tile([P, JOINTS * K], BF16)
@@ -42,8 +40,8 @@ def tile_skeletonlinear_pa_s_kernel(tc, x, w_self, w_parent, bias, grad_out, out
         g_scales = keep.tile([P, JOINTS, P], U8, align_bytes=64)
         w_raw = keep.tile([P, JOINTS, 2, K], BF16)
         w_grouped = keep.tile([P, JOINTS, 2, BLOCK, PACK], BF16, align_bytes=64)
-        w_codes = keep.tile([P, JOINTS * PERIOD], U32, align_bytes=64)
-        w_scales = keep.tile([P, JOINTS * PERIOD], U8, align_bytes=64)
+        w_codes = keep.tile([P, LEAD + JOINTS * PERIOD], U32, align_bytes=64)
+        w_scales = keep.tile([P, LEAD + JOINTS * PERIOD], U8, align_bytes=64)
         out_sb = keep.tile([P, JOINTS * BLOCK], F32)
         identity = keep.tile([P, P], F32)
 
@@ -60,10 +58,11 @@ def tile_skeletonlinear_pa_s_kernel(tc, x, w_self, w_parent, bias, grad_out, out
                 in_=w_self[first : first + 2].rearrange("n (p t) i -> p n (t i)", t=PACK),
             )
 
-        code_gaps = w_codes[:].bitcast(I32).rearrange("p (n w) -> p n w", w=PERIOD)
-        nc.vector.memset(code_gaps[:, 0 : JOINTS - 1, 2 * BLOCK : PERIOD], 0)
-        scale_gaps = w_scales[:].bitcast(I32).rearrange("p (n w) -> p n w", w=PERIOD // 4)
-        nc.vector.memset(scale_gaps[:, 0 : JOINTS - 1, 2 * BLOCK // 4 : PERIOD // 4], 0)
+        for row, per_word in ((w_codes, 1), (w_scales, 4)):
+            words = row[:].bitcast(I32)
+            nc.vector.memset(words[:, 0 : (LEAD + BLOCK) // per_word], 0)
+            joints = words[:, LEAD // per_word :].rearrange("p (n w) -> p n w", n=JOINTS)
+            nc.vector.memset(joints[:, :, 2 * BLOCK // per_word :], 0)
         make_identity(nc, identity[:])
 
         g_words = g_raw[:].bitcast(F32).rearrange("b (n q u) -> b n u q", n=JOINTS, u=2)
@@ -83,15 +82,15 @@ def tile_skeletonlinear_pa_s_kernel(tc, x, w_self, w_parent, bias, grad_out, out
             )
 
         def group_w(first):
-            pair = slice(first, first + 2)
+            blocks = slice(PARENT if first > 0 else SELF, SELF + 1)
             nc.vector.tensor_copy(
-                out=w_grouped[:, pair, SELF].rearrange("p n (c r) t -> p n c t r", r=4),
-                in_=w_raw[:, pair, SELF].rearrange("p n (t c r) -> p n c t r", t=PACK, r=4),
+                out=w_grouped[:, first, blocks].rearrange("p s (c r) t -> p s c t r", r=4),
+                in_=w_raw[:, first, blocks].rearrange("p s (t c r) -> p s c t r", t=PACK, r=4),
             )
-            for n in range(max(first, 1), first + 2):
-                nc.scalar.copy(
-                    out=w_grouped[:, n, PARENT].rearrange("p (c r) t -> p c t r", r=4),
-                    in_=w_raw[:, n, PARENT].rearrange("p (t c r) -> p c t r", t=PACK, r=4),
+            for engine_copy, s in ((nc.vector.tensor_copy, SELF), (nc.scalar.copy, PARENT)):
+                engine_copy(
+                    out=w_grouped[:, first + 1, s].rearrange("p (c r) t -> p c t r", r=4),
+                    in_=w_raw[:, first + 1, s].rearrange("p (t c r) -> p c t r", t=PACK, r=4),
                 )
 
         def quantise_g(first):
@@ -104,15 +103,16 @@ def tile_skeletonlinear_pa_s_kernel(tc, x, w_self, w_parent, bias, grad_out, out
 
         def quantise_w(n):
             blocks = slice(PARENT if n > 0 else SELF, SELF + 1)
-            cols = slice(n * PERIOD + (0 if n > 0 else BLOCK), n * PERIOD + 2 * BLOCK)
+            self_col = LEAD + n * PERIOD + BLOCK
+            cols = slice(self_col - (BLOCK if n > 0 else 0), self_col + BLOCK)
             nc.vector.quantize_mx(
                 out=w_codes[:, cols].bitcast(E4M3_X4),
                 scales=w_scales[:, cols],
                 in_=w_grouped[:, n, blocks].rearrange("p s i t -> p (s i t)"),
             )
 
-        def multiply(acc, n, first_col, start, stop):
-            window = slice(first_col, first_col + WINDOW)
+        def multiply(acc, n, last_col, start, stop):
+            window = slice(last_col - WINDOW, last_col)
             nc.tensor.matmul_mx(
                 out=acc[:],
                 lhsT=g_codes[:, n, :].bitcast(E5M2_X4),
@@ -123,9 +123,9 @@ def tile_skeletonlinear_pa_s_kernel(tc, x, w_self, w_parent, bias, grad_out, out
                 stop=stop,
             )
 
-        def store(acc, bank):
-            cols = slice(bank * WINDOW, (bank + 1) * WINDOW)
-            nc.vector.tensor_copy(out=out_sb[:, cols], in_=acc[:])
+        def store(acc, first):
+            cols = slice(first * BLOCK, (first + 2) * BLOCK)
+            nc.scalar.copy(out=out_sb[:, cols], in_=acc[:, UNREAD:WINDOW])
             nc.sync.dma_start(out=out[:, cols], in_=out_sb[:, cols])
 
         acc = None
@@ -139,17 +139,16 @@ def tile_skeletonlinear_pa_s_kernel(tc, x, w_self, w_parent, bias, grad_out, out
             if first + 2 < JOINTS:
                 group_g(first + 2, turned)
             if full is not None:
-                store(full, first // BANK_JOINTS - 1)
-                full = None
+                store(full, first - 4)
             quantise_g(first)
-            for n in (first, first + 1):
-                quantise_w(n)
-                place = n % BANK_JOINTS
-                self_col = n * PERIOD + BLOCK
-                if place == 0:
-                    if n > 0:
-                        multiply(acc, n, self_col - WINDOW, start=False, stop=True)
-                        full = acc
-                    acc = acc_psum.tile([P, WINDOW], F32)
-                multiply(acc, n, self_col - place * BLOCK, start=(place == 0), stop=(n == JOINTS - 1))
-        store(acc, BANKS - 1)
+            quantise_w(first)
+            quantise_w(first + 1)
+            self_end = LEAD + first * PERIOD + 2 * BLOCK
+            if first > 0:
+                multiply(acc, first, self_end - BLOCK, start=False, stop=True)
+                full = acc
+            acc = acc_psum.tile([P, WINDOW], F32)
+            multiply(acc, first, self_end + BLOCK, start=True, stop=False)
+            multiply(acc, first + 1, self_end + PERIOD, start=False, stop=(first + 2 == JOINTS))
+        store(full, JOINTS - 4)
+        store(acc, JOINTS - 2)

@@ -82,16 +82,17 @@ def tile_skeletonlinear_pa_s_kernel(tc, x, w_self, w_parent, bias, grad_out, out
             )
 
         def group_w(first):
-            blocks = slice(PARENT if first > 0 else SELF, SELF + 1)
+            for engine_copy, n in ((nc.vector.tensor_copy, first), (nc.scalar.copy, first + 1)):
+                if n > 0:
+                    engine_copy(
+                        out=w_grouped[:, n, PARENT].rearrange("p (c r) t -> p c t r", r=4),
+                        in_=w_raw[:, n, PARENT].rearrange("p (t c r) -> p c t r", t=PACK, r=4),
+                    )
+            pair = slice(first, first + 2)
             nc.vector.tensor_copy(
-                out=w_grouped[:, first, blocks].rearrange("p s (c r) t -> p s c t r", r=4),
-                in_=w_raw[:, first, blocks].rearrange("p s (t c r) -> p s c t r", t=PACK, r=4),
+                out=w_grouped[:, pair, SELF].rearrange("p n (c r) t -> p n c t r", r=4),
+                in_=w_raw[:, pair, SELF].rearrange("p n (t c r) -> p n c t r", t=PACK, r=4),
             )
-            for engine_copy, s in ((nc.vector.tensor_copy, SELF), (nc.scalar.copy, PARENT)):
-                engine_copy(
-                    out=w_grouped[:, first + 1, s].rearrange("p (c r) t -> p c t r", r=4),
-                    in_=w_raw[:, first + 1, s].rearrange("p (t c r) -> p c t r", t=PACK, r=4),
-                )
 
         def quantise_g(first):
             pair = slice(first, first + 2)
@@ -136,10 +137,10 @@ def tile_skeletonlinear_pa_s_kernel(tc, x, w_self, w_parent, bias, grad_out, out
             if first + 2 < JOINTS:
                 turned = transpose_g(first + 2)
             group_w(first)
-            if first + 2 < JOINTS:
-                group_g(first + 2, turned)
             if full is not None:
                 store(full, first - 4)
+            if first + 2 < JOINTS:
+                group_g(first + 2, turned)
             quantise_g(first)
             quantise_w(first)
             quantise_w(first + 1)

@@ -82,12 +82,15 @@ def tile_skeletonlinear_pa_s_kernel(tc, x, w_self, w_parent, bias, grad_out, out
             )
 
         def group_w(first):
-            for engine_copy, n in ((nc.vector.tensor_copy, first), (nc.scalar.copy, first + 1)):
-                if n > 0:
-                    engine_copy(
-                        out=w_grouped[:, n, PARENT].rearrange("p (c r) t -> p c t r", r=4),
-                        in_=w_raw[:, n, PARENT].rearrange("p (t c r) -> p c t r", t=PACK, r=4),
-                    )
+            if first > 0:
+                nc.vector.tensor_copy(
+                    out=w_grouped[:, first, PARENT].rearrange("p (c r) t -> p c t r", r=4),
+                    in_=w_raw[:, first, PARENT].rearrange("p (t c r) -> p c t r", t=PACK, r=4),
+                )
+            nc.scalar.copy(
+                out=w_grouped[:, first + 1, PARENT],
+                in_=w_raw[:, first + 1, PARENT].rearrange("p (t i) -> p i t", t=PACK),
+            )
             pair = slice(first, first + 2)
             nc.vector.tensor_copy(
                 out=w_grouped[:, pair, SELF].rearrange("p n (c r) t -> p n c t r", r=4),

from contextlib import ExitStack

import concourse.mybir as mybir
from concourse.masks import make_identity

BF16 = mybir.dt.bfloat16
F32 = mybir.dt.float32
I32 = mybir.dt.int32
U32 = mybir.dt.uint32
U8 = mybir.dt.uint8
E4M3_X4 = mybir.dt.float8_e4m3fn_x4
E5M2_X4 = mybir.dt.float8_e5m2_x4

P = 128
PACK = 4
JOINTS = 12
K = P * PACK
BLOCK = 128
WINDOW = 4 * BLOCK
PERIOD = 3 * BLOCK
LEAD = BLOCK
UNREAD = 2 * BLOCK
PARENT, SELF = 0, 1

FLOPS = 2 * P * K * BLOCK * (2 * JOINTS - 1)
BYTES = 2 * (2 * JOINTS - 1) * K * BLOCK + 2 * P * JOINTS * K + 4 * P * JOINTS * BLOCK


def tile_skeletonlinear_pa_s_kernel(tc, x, w_self, w_parent, bias, grad_out, out):
    nc = tc.nc
    with ExitStack() as ctx:
        keep = ctx.enter_context(tc.tile_pool(name="keep", bufs=1))
        turn_psum = ctx.enter_context(tc.psum_pool(name="turn_psum", bufs=4))
        acc_psum = ctx.enter_context(tc.psum_pool(name="acc_psum", bufs=4))
        ctx.enter_context(tc.manual_schedule())

        g_raw = keep.tile([P, JOINTS * K], BF16)
        g_grouped = keep.tile([P, JOINTS, P, PACK], BF16, align_bytes=64)
        g_codes = keep.tile([P, JOINTS, P], U32, align_bytes=64)
        g_scales = keep.tile([P, JOINTS, P], U8, align_bytes=64)
        w_raw = keep.tile([P, JOINTS, 2, K], BF16)
        w_grouped = keep.tile([P, JOINTS, 2, BLOCK, PACK], BF16, align_bytes=64)
        w_codes = keep.tile([P, LEAD + JOINTS * PERIOD], U32, align_bytes=64)
        w_scales = keep.tile([P, LEAD + JOINTS * PERIOD], U8, align_bytes=64)
        out_sb = keep.tile([P, JOINTS * BLOCK], F32)
        identity = keep.tile([P, P], F32)

        for first in range(0, JOINTS, 2):
            g_cols = slice(first * K, (first + 2) * K)
            nc.sync.dma_start(out=g_raw[:, g_cols], in_=grad_out[:, g_cols])
            has_parent = max(first, 1)
            nc.sync.dma_start(
                out=w_raw[:, has_parent : first + 2, PARENT, :],
                in_=w_parent[has_parent - 1 : first + 1].rearrange("n (p t) i -> p n (t i)", t=PACK),
            )
            nc.sync.dma_start(
                out=w_raw[:, first : first + 2, SELF, :],
                in_=w_self[first : first + 2].rearrange("n (p t) i -> p n (t i)", t=PACK),
            )

        for row, per_word in ((w_codes, 1), (w_scales, 4)):
            words = row[:].bitcast(I32)
            nc.vector.memset(words[:, 0 : (LEAD + BLOCK) // per_word], 0)
            joints = words[:, LEAD // per_word :].rearrange("p (n w) -> p n w", n=JOINTS)
            nc.vector.memset(joints[:, :, 2 * BLOCK // per_word :], 0)
        make_identity(nc, identity[:])

        g_words = g_raw[:].bitcast(F32).rearrange("b (n q u) -> b n u q", n=JOINTS, u=2)
        g_grouped_words = g_grouped[:].bitcast(F32)

        def transpose_g(first):
            turned = turn_psum.tile([P, 2, 2, P], F32)
            for j in range(2):
                for u in range(2):
                    nc.tensor.transpose(turned[:, j, u, :], g_words[:, first + j, u, :], identity[:])
            return turned

        def group_g(first, turned):
            nc.scalar.copy(
                out=g_grouped_words[:, first : first + 2, :, :],
                in_=turned[:].rearrange("p n u b -> p n b u"),
            )

        def group_w(first):
            if first > 0:
                nc.vector.tensor_copy(
                    out=w_grouped[:, first, PARENT].rearrange("p (c r) t -> p c t r", r=4),
                    in_=w_raw[:, first, PARENT].rearrange("p (t c r) -> p c t r", t=PACK, r=4),
                )
            nc.scalar.copy(
                out=w_grouped[:, first + 1, PARENT],
                in_=w_raw[:, first + 1, PARENT].rearrange("p (t i) -> p i t", t=PACK),
            )
            pair = slice(first, first + 2)
            nc.vector.tensor_copy(
                out=w_grouped[:, pair, SELF].rearrange("p n (c r) t -> p n c t r", r=4),
                in_=w_raw[:, pair, SELF].rearrange("p n (t c r) -> p n c t r", t=PACK, r=4),
            )

        def quantise_g(first):
            pair = slice(first, first + 2)
            nc.vector.quantize_mx(
                out=g_codes[:, pair, :].rearrange("p n b -> p (n b)").bitcast(E5M2_X4),
                scales=g_scales[:, pair, :].rearrange("p n b -> p (n b)"),
                in_=g_grouped[:, pair].rearrange("p n b t -> p (n b t)"),
            )

        def quantise_w(n):
            blocks = slice(PARENT if n > 0 else SELF, SELF + 1)
            self_col = LEAD + n * PERIOD + BLOCK
            cols = slice(self_col - (BLOCK if n > 0 else 0), self_col + BLOCK)
            nc.vector.quantize_mx(
                out=w_codes[:, cols].bitcast(E4M3_X4),
                scales=w_scales[:, cols],
                in_=w_grouped[:, n, blocks].rearrange("p s i t -> p (s i t)"),
            )

        def multiply(acc, n, last_col, start, stop):
            window = slice(last_col - WINDOW, last_col)
            nc.tensor.matmul_mx(
                out=acc[:],
                lhsT=g_codes[:, n, :].bitcast(E5M2_X4),
                lhsT_scale=g_scales[:, n, :],
                rhs=w_codes[:, window].bitcast(E4M3_X4),
                rhs_scale=w_scales[:, window],
                start=start,
                stop=stop,
            )

        def store(acc, first):
            cols = slice(first * BLOCK, (first + 2) * BLOCK)
            nc.scalar.copy(out=out_sb[:, cols], in_=acc[:, UNREAD:WINDOW])
            nc.sync.dma_start(out=out[:, cols], in_=out_sb[:, cols])

        acc = None
        full = None
        turned = transpose_g(0)
        group_g(0, turned)
        for first in range(0, JOINTS, 2):
            if first + 2 < JOINTS:
                turned = transpose_g(first + 2)
            group_w(first)
            if full is not None:
                store(full, first - 4)
            if first + 2 < JOINTS:
                group_g(first + 2, turned)
            quantise_g(first)
            quantise_w(first)
            quantise_w(first + 1)
            self_end = LEAD + first * PERIOD + 2 * BLOCK
            if first > 0:
                multiply(acc, first, self_end - BLOCK, start=False, stop=True)
                full = acc
            acc = acc_psum.tile([P, WINDOW], F32)
            multiply(acc, first, self_end + BLOCK, start=True, stop=False)
            multiply(acc, first + 1, self_end + PERIOD, start=False, stop=(first + 2 == JOINTS))
        store(full, JOINTS - 4)
        store(acc, JOINTS - 2)
